import numpy as np
import ml_dtypes


def mxq(x, axis, fmt="e4m3"):
    dtype, down = {"e4m3": (ml_dtypes.float8_e4m3fn, 7), "e5m2": (ml_dtypes.float8_e5m2, 14)}[fmt]
    v = np.moveaxis(np.asarray(x, np.float32).astype(ml_dtypes.bfloat16).astype(np.float64), axis, -1)
    blocks = v.reshape(v.shape[:-1] + (-1, 32))
    amax = np.abs(blocks).max(-1, keepdims=True)
    byte = np.maximum(np.where(amax > 0, np.frexp(amax)[1] - 1 + 127, 0) - down, 1)
    scale = np.exp2(byte - 127.0)
    codes = (blocks / scale).astype(np.float32).astype(dtype).astype(np.float64)
    return np.moveaxis((codes * scale).reshape(v.shape), -1, axis)


WIDE = False


def mx_kscale(k):
    if not WIDE:
        return np.ones(k)
    levels = np.array([10, -10, 5, -5, 0])
    if k % 512:
        return np.exp2(np.random.permutation(np.resize(levels, k // 32))).repeat(32)
    a = np.empty((k // 512, 16))
    for p in range(k // 512):
        a[p, :8] = np.random.permutation(np.resize(levels, 8))
        for g in range(8):
            far = levels[np.abs(levels - a[p, g]) >= 10]
            a[p, g + 8] = far[np.random.randint(len(far))]
    return np.exp2(a.ravel()).repeat(32)


BF16 = ml_dtypes.bfloat16


def bf(x):
    return np.asarray(x, np.float32).astype(BF16)


def f64(x):
    return np.asarray(x).astype(np.float64)


B, F, H, C = 1024, 1024, 512, 10
EPS = 4.0 / 30.0
P_KEEP = 0.95


def draw0():
    s = mx_kscale(F)
    ns = EPS / (6.0 * np.sqrt(H))
    return {"x1": bf(np.random.standard_normal((B, F)) * s),
            "x2": bf(np.random.standard_normal((B, F)) * s),
            "W1": bf(np.random.standard_normal((F, H)) / np.sqrt(F) / s[:, None]),
            "b1": bf(np.random.standard_normal(H) * 0.3),
            "W2": bf(np.random.standard_normal((F, H)) / np.sqrt(F) / s[:, None]),
            "b2": bf(np.random.standard_normal(H) * 0.3),
            "noise_std": bf(np.random.laplace(size=(B, H)) * ns),
            "rr_uniform": bf(np.random.uniform(size=H))}


def core(x1, x2, W1, b1, W2, b2, noise_std, rr_uniform):
    out1 = (mxq(f64(x1), 1, "e4m3") @ mxq(f64(W1), 0, "e4m3")) + f64(b1)
    one_norm = np.sum(np.abs(out1), axis=1)
    sensitivity = np.max(one_norm) - np.min(one_norm)
    noise_mul = sensitivity / EPS
    out1 = out1 + f64(noise_std) * noise_mul
    rr_mask = np.where(f64(rr_uniform) < P_KEEP, 1.0, 0.0)
    out1 = out1 * rr_mask
    out2 = (mxq(f64(x2), 1, "e4m3") @ mxq(f64(W2), 0, "e4m3")) + f64(b2)
    return np.minimum(out1, out2)


def e4m3fn_bytes(y):
    return np.clip(np.asarray(y, np.float64), -448.0, 448.0).astype(np.float32).astype(ml_dtypes.float8_e4m3fn).view(np.uint8)


def e4m3fn_values(b):
    return np.asarray(b, np.uint8).view(ml_dtypes.float8_e4m3fn).astype(np.float64)


def setup_inputs():
    d = draw0()
    x0 = np.asarray(d['x2']).astype(np.float64)
    s = (np.max(np.abs(x0), axis=(0,), keepdims=True) / 448.0).astype(np.float32)
    out = {}
    for k, v in d.items():
        if k == 'x2':
            out['x2_bytes'] = e4m3fn_bytes(x0 / s.astype(np.float64))
            out['x2_scale'] = s
        else:
            out[k] = v
    return out


def reference(x1, x2_bytes, x2_scale, W1, b1, W2, b2, noise_std, rr_uniform):
    return core(x1, e4m3fn_values(x2_bytes) * x2_scale.astype(np.float64), W1, b1, W2, b2, noise_std, rr_uniform)

@@ -1,0 +1,406 @@
+from contextlib import ExitStack
+
+import concourse.mybir as mybir
+from concourse.masks import make_identity
+
+ROWS, K, CH = 1024, 1024, 512
+FLOPS = 2 * 2 * ROWS * K * CH
+
+F32 = mybir.dt.float32
+BF16 = mybir.dt.bfloat16
+U32 = mybir.dt.uint32
+U8 = mybir.dt.uint8
+FP8 = mybir.dt.float8_e4m3fn
+FP8X4 = mybir.dt.float8_e4m3fn_x4
+ALU = mybir.AluOpType
+ACT = mybir.ActivationFunctionType
+AX = mybir.AxisListType
+
+P = 128
+PACK = 4
+K_PASS = P * PACK
+PASSES = K // K_PASS
+HALF = 512
+HALVES = ROWS // HALF
+RT = HALF // P
+CT = CH // P
+NT = ROWS // P
+INV_EPS = 30.0 / 4.0
+P_KEEP = 0.95
+
+
+def tile_splitnn_pa_kernel(tc, x1, x2_bytes, x2_scale, W1, b1, W2, b2, noise_std, rr_uniform, out):
+    nc = tc.nc
+    with ExitStack() as ctx:
+        keep = ctx.enter_context(tc.tile_pool(name="keep", bufs=1))
+        rot = ctx.enter_context(tc.tile_pool(name="rot", bufs=2))
+        psum = ctx.enter_context(tc.psum_pool(name="psum", bufs=8))
+        ctx.enter_context(tc.manual_schedule())
+
+        def bank(shape, dtype):
+            t = psum.tile(shape, dtype, name="bank", tag="bank", bufs=8)
+            return t
+
+        x1_v = x1.rearrange("(p a) k -> p a k", a=NT)
+        xb_v = x2_bytes.rearrange("(p a) k -> p a k", a=NT)
+        nz_v = noise_std.rearrange("(p a) c -> p a c", a=NT)
+        out_v = out.rearrange("(p a) c -> p a c", a=NT)
+
+        srow = keep.tile([P, P], F32, name="srow")
+        nc.gpsimd.memset(srow[:], 0.0)
+        vrow = keep.tile([P, P], BF16, name="vrow")
+        nc.gpsimd.memset(vrow[:], 0.0)
+        warm = keep.tile([P, 2], F32, name="warm")
+        nc.vector.memset(warm[:], 0.0)
+        nc.scalar.activation(out=warm[:, 1:2], in_=warm[:, 0:1], func=ACT.Abs)
+        ident_f = keep.tile([P, P], F32, name="ident_f")
+        make_identity(nc, ident_f[:])
+        ident_b = keep.tile([P, P], BF16, name="ident_b")
+        make_identity(nc, ident_b[:])
+
+        weights = (W1, W2)
+        wraw = {}
+        x1sb = keep.tile([P, NT, K], BF16, name="x1sb")
+        xbytes = keep.tile([P, NT, K], U8, name="x2bytes")
+        noise = keep.tile([P, NT, CH], BF16, name="noise")
+
+        def load_w(w, g):
+            t = keep.tile([P, PACK, CH], BF16, name="wraw%d%d" % (w, g))
+            wraw[(w, g)] = t
+            nc.sync.dma_start(out=t[:], in_=weights[w][g * K_PASS:(g + 1) * K_PASS, :].rearrange("(p j) c -> p j c", j=PACK))
+
+        def load_x1(a, n):
+            nc.sync.dma_start(out=x1sb[:, a:a + n, :], in_=x1_v[:, a:a + n, :])
+
+        def load_bytes(a, n):
+            nc.sync.dma_start(out=xbytes[:, a:a + n, :], in_=xb_v[:, a:a + n, :])
+
+        def load_noise(a, n):
+            nc.sync.dma_start(out=noise[:, a:a + n, :], in_=nz_v[:, a:a + n, :])
+
+        def load_small():
+            nc.sync.dma_start(out=srow[0:K // P, :], in_=x2_scale.rearrange("o (j n) -> (o j) n", n=P))
+            for j, vec in enumerate((b1, b2, rr_uniform)):
+                nc.sync.dma_start(out=vrow[CT * j:CT * (j + 1), :], in_=vec.rearrange("(c p) -> c p", p=P))
+
+        load_small()
+        load_w(0, 0)
+        load_w(1, 0)
+        load_bytes(0, 4)
+        load_x1(0, 2)
+        load_x1(2, 2)
+        load_w(0, 1)
+        load_x1(4, 2)
+        load_x1(6, 2)
+        load_bytes(4, 4)
+        load_w(1, 1)
+        load_noise(0, 4)
+        load_noise(4, 4)
+
+        scale_bc = keep.tile([P, K], F32, name="scale_bc")
+        scol = keep.tile([P, K // P], F32, name="scol")
+
+        def scale_cols():
+            t = bank([P, P], F32)
+            nc.tensor.transpose(t[:], srow[:], ident_f[:])
+            nc.scalar.copy(out=scol[:], in_=t[:, 0:K // P])
+
+        def scale_spread(s):
+            t = bank([P, RT, P], F32)
+            for j in range(RT):
+                nc.tensor.transpose(t[:, j, :], scol[:, s * RT + j:s * RT + j + 1].to_broadcast([P, P]), ident_f[:])
+            nc.scalar.copy(out=scale_bc[:, s * HALF:(s + 1) * HALF], in_=t[:].rearrange("p j n -> p (j n)"))
+
+        vcol = keep.tile([P, 3 * CT], F32, name="vcol")
+        b1c = vcol[:, 0:CT]
+        b2c = vcol[:, CT:2 * CT]
+        keepc = keep.tile([P, CT], F32, name="keepc")
+        b1k = keep.tile([P, CT], F32, name="b1k")
+
+        def vec_prep():
+            vps = bank([P, P], BF16)
+            nc.tensor.transpose(vps[:], vrow[:], ident_b[:])
+            nc.scalar.copy(out=vcol[:], in_=vps[:, 0:3 * CT])
+            nc.gpsimd.tensor_scalar(out=keepc[:], in0=vcol[:, 2 * CT:3 * CT], scalar1=P_KEEP, scalar2=None, op0=ALU.is_lt)
+            nc.gpsimd.tensor_tensor(out=b1k[:], in0=b1c, in1=keepc[:], op=ALU.mult)
+
+        wcodes = []
+        wscl = []
+        wgrp = {}
+        for w in range(2):
+            wc = keep.tile([P, PASSES, CH], U32, name="wcodes%d" % w, align_bytes=64)
+            ws = keep.tile([P, PASSES, CH], U8, name="wscl%d" % w, align_bytes=64)
+            wcodes.append(wc)
+            wscl.append(ws)
+            for g in range(PASSES):
+                wg = keep.tile([P, CH, PACK], BF16, name="wgrp%d%d" % (w, g), align_bytes=64)
+                wgrp[(w, g)] = wg
+        xgrp = {}
+        xcodes = {}
+        xscl = {}
+        for w in range(2):
+            for h in range(HALVES):
+                xg = keep.tile([P, PASSES, HALF, PACK], BF16, name="xgrp%d%d" % (w, h), align_bytes=64)
+                xc = keep.tile([P, PASSES, HALF], U32, name="xcodes%d%d" % (w, h), align_bytes=64)
+                xs = keep.tile([P, PASSES, HALF], U8, name="xscl%d%d" % (w, h), align_bytes=64)
+                xgrp[(w, h)] = xg
+                xcodes[(w, h)] = xc
+                xscl[(w, h)] = xs
+
+        def w_lace(w, g, eng):
+            src = wraw[(w, g)][:].rearrange("p j (c i) -> p c j i", i=4)
+            dst = wgrp[(w, g)][:].rearrange("p (c i) j -> p c j i", i=4)
+            if eng == "V":
+                nc.vector.tensor_copy(out=dst, in_=src)
+            else:
+                nc.scalar.copy(out=dst, in_=src)
+
+        def w_quant(w, g):
+            nc.vector.quantize_mx(out=wcodes[w][:, g, :].bitcast(FP8X4), scales=wscl[w][:, g, :],
+                                  in_=wgrp[(w, g)][:].rearrange("p c j -> p (c j)"))
+
+        xt = {}
+        x2bf = keep.tile([P, NT, K], BF16, name="x2bf")
+
+        def widen(a):
+            nc.vector.tensor_tensor(out=x2bf[:, a, :], in0=xbytes[:, a, :].bitcast(FP8), in1=scale_bc[:], op=ALU.mult)
+
+        def x_turn(w, a):
+            src = x1sb if w == 0 else x2bf
+            words = src[:, a, :].bitcast(F32)
+            t = bank([P, PASSES, 2, P], F32)
+            for g in range(PASSES):
+                for u in range(2):
+                    nc.tensor.transpose(t[:, g, u, :], words[:, 256 * g + u:256 * (g + 1):2], ident_f[:])
+            xt[(w, a)] = t
+
+        def x_copy(w, a, eng="S"):
+            h, i = divmod(a, RT)
+            dst = xgrp[(w, h)][:].bitcast(F32)[:, :, i * P:(i + 1) * P, :]
+            src = xt[(w, a)][:].rearrange("p g u r -> p g r u")
+            if eng == "V":
+                nc.vector.tensor_copy(out=dst, in_=src)
+            else:
+                nc.scalar.copy(out=dst, in_=src)
+
+        def x_quant(w, h):
+            nc.vector.quantize_mx(out=xcodes[(w, h)][:].rearrange("p g r -> p (g r)").bitcast(FP8X4),
+                                  scales=xscl[(w, h)][:].rearrange("p g r -> p (g r)"),
+                                  in_=xgrp[(w, h)][:].rearrange("p g r t -> p (g r t)"))
+
+        acc = {}
+
+        def mx(w, h, c):
+            t = bank([P, HALF], F32)
+            for g in range(PASSES):
+                nc.tensor.matmul_mx(out=t[:],
+                                    lhsT=wcodes[w][:, g, c * P:(c + 1) * P].bitcast(FP8X4),
+                                    lhsT_scale=wscl[w][:, g, c * P:(c + 1) * P],
+                                    rhs=xcodes[(w, h)][:, g, :].bitcast(FP8X4),
+                                    rhs_scale=xscl[(w, h)][:, g, :],
+                                    start=(g == 0), stop=(g == PASSES - 1))
+            acc[(w, h, c)] = t
+
+        absT = {}
+        akT = {}
+
+        def c1_abs(h, c):
+            ab = rot.tile([P, HALF], F32, name="absT", tag="absT", bufs=8)
+            nc.scalar.activation(out=ab[:], in_=acc[(0, h, c)][:], func=ACT.Abs, bias=b1c[:, c:c + 1], scale=1.0)
+            absT[(h, c)] = ab
+
+        def c1_keep(h, c, eng="S"):
+            ak = keep.tile([P, HALF], F32, name="akT%d%d" % (h, c))
+            if eng == "V":
+                nc.vector.tensor_scalar(out=ak[:], in0=acc[(0, h, c)][:], scalar1=keepc[:, c:c + 1], scalar2=b1k[:, c:c + 1],
+                                        op0=ALU.mult, op1=ALU.add)
+            else:
+                nc.scalar.activation(out=ak[:], in_=acc[(0, h, c)][:], func=ACT.Identity, bias=b1k[:, c:c + 1],
+                                     scale=keepc[:, c:c + 1])
+            akT[(h, c)] = ak
+
+        nsum = keep.tile([P, NT], F32, name="nsum")
+        nps = {}
+
+        def norm_turn(h):
+            t = bank([P, RT, P], F32)
+            for i in range(RT):
+                for c in range(CT):
+                    nc.tensor.matmul(out=t[:, i, :], lhsT=absT[(h, c)][:, i * P:(i + 1) * P], rhs=ident_f[:],
+                                     is_transpose=True, start=(c == 0), stop=(c == CT - 1))
+            nps[h] = t
+
+        def norm_sum(h):
+            nc.vector.tensor_reduce(out=nsum[:, h * RT:(h + 1) * RT], in_=nps[h][:], axis=AX.X, op=ALU.add)
+
+        mulk = keep.tile([P, CT], F32, name="mulk")
+        nmx = keep.tile([P, 2], F32, name="nmx")
+        spr = {}
+
+        def barrier_a():
+            nc.vector.tensor_reduce(out=nmx[:, 0:1], in_=nsum[:], axis=AX.X, op=ALU.max)
+            nc.vector.tensor_reduce(out=nmx[:, 1:2], in_=nsum[:], axis=AX.X, op=ALU.min)
+            t = bank([P, 2, P], F32)
+            for j in range(2):
+                nc.tensor.matmul(out=t[:, j, :], lhsT=nmx[:, j:j + 1].to_broadcast([P, P]), rhs=ident_f[:],
+                                 start=True, stop=True)
+            spr[0] = t
+
+        def barrier_b():
+            spread = spr[0]
+            ext = keep.tile([P, 2], F32, name="ext")
+            nc.vector.tensor_reduce(out=ext[:, 0:1], in_=spread[:, 0, :], axis=AX.X, op=ALU.max)
+            nc.vector.tensor_reduce(out=ext[:, 1:2], in_=spread[:, 1, :], axis=AX.X, op=ALU.min)
+            mul = keep.tile([P, 1], F32, name="mul")
+            nc.vector.tensor_scalar(out=mul[:], in0=ext[:, 0:1], scalar1=ext[:, 1:2], scalar2=INV_EPS,
+                                    op0=ALU.subtract, op1=ALU.mult)
+            nc.vector.tensor_scalar(out=mulk[:], in0=keepc[:], scalar1=mul[:, 0:1], scalar2=None, op0=ALU.mult)
+
+        nT = {}
+        cT = {}
+        oT = {}
+        ob = {}
+        osb = {}
+
+        def noise_turn(h, c0):
+            t = bank([P, 2, HALF], BF16)
+            for c in (c0, c0 + 1):
+                for i in range(RT):
+                    nc.tensor.transpose(t[:, c - c0, i * P:(i + 1) * P], noise[:, h * RT + i, c * P:(c + 1) * P], ident_b[:])
+                nT[(h, c)] = t[:, c - c0, :]
+
+        def noise_out(h, c0):
+            t = keep.tile([P, 2, HALF], BF16, name="nsb%d%d" % (h, c0))
+            nc.scalar.copy(out=t[:, 0, :], in_=nT[(h, c0)])
+            nc.scalar.copy(out=t[:, 1, :], in_=nT[(h, c0 + 1)])
+            nT[(h, c0)] = t[:, 0, :]
+            nT[(h, c0 + 1)] = t[:, 1, :]
+
+        def c_make(h, c):
+            t = rot.tile([P, HALF], F32, name="cT", tag="cT", bufs=8)
+            nc.vector.scalar_tensor_tensor(out=t[:], in0=nT[(h, c)], scalar=mulk[:, c:c + 1], in1=akT[(h, c)][:],
+                                           op0=ALU.mult, op1=ALU.add)
+            cT[(h, c)] = t
+
+        def o_make(h, c, q=0, n=HALF):
+            if (h, c) not in oT:
+                t = rot.tile([P, HALF], F32, name="oT", tag="oT", bufs=8)
+                oT[(h, c)] = t
+            nc.vector.scalar_tensor_tensor(out=oT[(h, c)][:, q * n:(q + 1) * n], in0=acc[(1, h, c)][:, q * n:(q + 1) * n],
+                                           scalar=b2c[:, c:c + 1], in1=cT[(h, c)][:, q * n:(q + 1) * n],
+                                           op0=ALU.add, op1=ALU.min)
+
+        def o_turn(h, i, cs):
+            if (h, i) not in ob:
+                t = bank([P, CH], F32)
+                ob[(h, i)] = t
+            for c in cs:
+                nc.tensor.transpose(ob[(h, i)][:, c * P:(c + 1) * P], oT[(h, c)][:, i * P:(i + 1) * P], ident_f[:])
+
+        def o_out(h, i, eng):
+            a = h * RT + i
+            if a // 2 not in osb:
+                t = keep.tile([P, 2, CH], F32, name="osb%d" % (a // 2))
+                osb[a // 2] = t
+            if eng == "V":
+                nc.vector.tensor_copy(out=osb[a // 2][:, a % 2, :], in_=ob[(h, i)][:])
+            else:
+                nc.scalar.copy(out=osb[a // 2][:, a % 2, :], in_=ob[(h, i)][:])
+
+        def o_store(a, n):
+            nc.sync.dma_start(out=out_v[:, a:a + n, :], in_=osb[a // 2][:, a % 2:a % 2 + n, :])
+
+        w_lace(0, 0, "V")
+        scale_cols()
+        scale_spread(0)
+        scale_spread(1)
+        w_quant(0, 0)
+        w_lace(1, 0, "S")
+        widen(0)
+        widen(1)
+        widen(2)
+        for a in range(NT):
+            x_turn(0, a)
+        for a in range(RT):
+            x_copy(0, a)
+        w_lace(0, 1, "V")
+        x_quant(0, 0)
+        w_quant(0, 1)
+        for a in range(RT, NT):
+            x_copy(0, a)
+        vec_prep()
+        widen(3)
+        x_quant(0, 1)
+        for c in range(CT):
+            mx(0, 0, c)
+        c1_abs(0, 0)
+        c1_keep(0, 0)
+        c1_abs(0, 1)
+        c1_keep(0, 1)
+        c1_abs(0, 2)
+        c1_abs(0, 3)
+        widen(4)
+        w_lace(1, 1, "V")
+        c1_keep(0, 2, "V")
+        for c in range(CT):
+            mx(0, 1, c)
+        norm_turn(0)
+        for c in range(CT):
+            c1_abs(1, c)
+        widen(5)
+        widen(6)
+        norm_sum(0)
+        norm_turn(1)
+        widen(7)
+        c1_keep(0, 3)
+        c1_keep(1, 0)
+        c1_keep(1, 1)
+        for a in range(RT):
+            x_turn(1, a)
+        norm_sum(1)
+        barrier_a()
+        w_quant(1, 0)
+        w_quant(1, 1)
+        for a in range(RT):
+            x_copy(1, a)
+        noise_turn(0, 0)
+        noise_turn(0, 2)
+        barrier_b()
+        c_make(0, 0)
+        x_quant(1, 0)
+        for a in range(RT, NT):
+            x_turn(1, a)
+        for a in range(RT, NT):
+            x_copy(1, a)
+        c_make(0, 1)
+        c_make(0, 2)
+        c_make(0, 3)
+        for c in range(CT):
+            mx(1, 0, c)
+        c1_keep(1, 2)
+        c1_keep(1, 3)
+        noise_turn(1, 0)
+        noise_turn(1, 2)
+        x_quant(1, 1)
+        for c in range(CT):
+            o_make(0, c)
+        mx(1, 1, 0)
+        mx(1, 1, 1)
+        for c in range(CT):
+            c_make(1, c)
+        for i in range(RT):
+            o_turn(0, i, range(CT))
+            o_out(0, i, "S")
+            if i % 2 == 1:
+                o_store(i - 1, 2)
+        mx(1, 1, 2)
+        mx(1, 1, 3)
+        for q in range(2):
+            for c in range(CT):
+                o_make(1, c, q, 256)
+                o_turn(1, 2 * q, [c])
+                o_turn(1, 2 * q + 1, [c])
+            o_out(1, 2 * q, "S")
+            o_store(RT + 2 * q, 1)
+            o_out(1, 2 * q + 1, "S" if q == 0 else "V")
+            o_store(RT + 2 * q + 1, 1)

@@ -85,14 +85,15 @@ def tile_splitnn_pa_kernel(tc, x1, x2_bytes, x2_scale, W1, b1, W2, b2, noise_std
 
         load_small()
         load_w(0, 0)
-        load_w(1, 0)
         load_bytes(0, 4)
         load_x1(0, 2)
         load_x1(2, 2)
         load_w(0, 1)
         load_x1(4, 2)
-        load_x1(6, 2)
+        load_x1(6, 1)
+        load_x1(7, 1)
         load_bytes(4, 4)
+        load_w(1, 0)
         load_w(1, 1)
         load_noise(0, 4)
         load_noise(4, 4)
@@ -147,9 +148,9 @@ def tile_splitnn_pa_kernel(tc, x1, x2_bytes, x2_scale, W1, b1, W2, b2, noise_std
                 xcodes[(w, h)] = xc
                 xscl[(w, h)] = xs
 
-        def w_lace(w, g, eng):
-            src = wraw[(w, g)][:].rearrange("p j (c i) -> p c j i", i=4)
-            dst = wgrp[(w, g)][:].rearrange("p (c i) j -> p c j i", i=4)
+        def w_lace(w, g, eng, c0=0, n=CH):
+            src = wraw[(w, g)][:, :, c0:c0 + n].rearrange("p j (c i) -> p c j i", i=4)
+            dst = wgrp[(w, g)][:, c0:c0 + n, :].rearrange("p (c i) j -> p c j i", i=4)
             if eng == "V":
                 nc.vector.tensor_copy(out=dst, in_=src)
             else:
@@ -187,6 +188,11 @@ def tile_splitnn_pa_kernel(tc, x1, x2_bytes, x2_scale, W1, b1, W2, b2, noise_std
             nc.vector.quantize_mx(out=xcodes[(w, h)][:].rearrange("p g r -> p (g r)").bitcast(FP8X4),
                                   scales=xscl[(w, h)][:].rearrange("p g r -> p (g r)"),
                                   in_=xgrp[(w, h)][:].rearrange("p g r t -> p (g r t)"))
+
+        def x_quant_rows(w, h, r0, n):
+            for g in range(PASSES):
+                nc.vector.quantize_mx(out=xcodes[(w, h)][:, g, r0:r0 + n].bitcast(FP8X4), scales=xscl[(w, h)][:, g, r0:r0 + n],
+                                      in_=xgrp[(w, h)][:, g, r0:r0 + n, :].rearrange("p r t -> p (r t)"))
 
         acc = {}
 
@@ -242,8 +248,7 @@ def tile_splitnn_pa_kernel(tc, x1, x2_bytes, x2_scale, W1, b1, W2, b2, noise_std
             nc.vector.tensor_reduce(out=nmx[:, 1:2], in_=nsum[:], axis=AX.X, op=ALU.min)
             t = bank([P, 2, P], F32)
             for j in range(2):
-                nc.tensor.matmul(out=t[:, j, :], lhsT=nmx[:, j:j + 1].to_broadcast([P, P]), rhs=ident_f[:],
-                                 start=True, stop=True)
+                nc.tensor.transpose(t[:, j, :], nmx[:, j:j + 1].to_broadcast([P, P]), ident_f[:])
             spr[0] = t
 
         def barrier_b():
@@ -315,7 +320,6 @@ def tile_splitnn_pa_kernel(tc, x1, x2_bytes, x2_scale, W1, b1, W2, b2, noise_std
         scale_spread(0)
         scale_spread(1)
         w_quant(0, 0)
-        w_lace(1, 0, "S")
         widen(0)
         widen(1)
         widen(2)
@@ -330,15 +334,18 @@ def tile_splitnn_pa_kernel(tc, x1, x2_bytes, x2_scale, W1, b1, W2, b2, noise_std
             x_copy(0, a)
         vec_prep()
         widen(3)
-        x_quant(0, 1)
+        x_quant_rows(0, 1, 0, 2 * P)
+        x_quant_rows(0, 1, 2 * P, 2 * P)
         for c in range(CT):
             mx(0, 0, c)
         c1_abs(0, 0)
         c1_keep(0, 0)
         c1_abs(0, 1)
+        w_lace(1, 0, "S", 0, P)
         c1_keep(0, 1)
         c1_abs(0, 2)
         c1_abs(0, 3)
+        w_lace(1, 0, "S", P, P)
         widen(4)
         w_lace(1, 1, "V")
         c1_keep(0, 2, "V")
@@ -347,6 +354,8 @@ def tile_splitnn_pa_kernel(tc, x1, x2_bytes, x2_scale, W1, b1, W2, b2, noise_std
         norm_turn(0)
         for c in range(CT):
             c1_abs(1, c)
+            if c % 2 == 1:
+                w_lace(1, 0, "S", (c + 3) // 2 * P, P)
         widen(5)
         widen(6)
         norm_sum(0)

@@ -271,7 +271,7 @@ def tile_splitnn_pa_kernel(tc, x1, x2_bytes, x2_scale, W1, b1, W2, b2, noise_std
             t = bank([P, 2, HALF], BF16)
             for c in (c0, c0 + 1):
                 for i in range(RT):
-                    nc.tensor.transpose(t[:, c - c0, i * P:(i + 1) * P], noise[:, h * RT + i, c * P:(c + 1) * P], ident_b[:])
+                    nc.tensor.matmul(out=t[:, c - c0, i * P:(i + 1) * P], lhsT=noise[:, h * RT + i, c * P:(c + 1) * P], rhs=ident_b[:])
                 nT[(h, c)] = t[:, c - c0, :]
 
         def noise_out(h, c0):

@@ -117,12 +117,14 @@ def tile_splitnn_pa_kernel(tc, x1, x2_bytes, x2_scale, W1, b1, W2, b2, noise_std
         b2c = vcol[:, CT:2 * CT]
         keepc = keep.tile([P, CT], F32, name="keepc")
         b1k = keep.tile([P, CT], F32, name="b1k")
+        keepe = keep.tile([P, CT], F32, name="keepe")
 
         def vec_prep():
             vps = bank([P, P], BF16)
             nc.tensor.transpose(vps[:], vrow[:], ident_b[:])
             nc.scalar.copy(out=vcol[:], in_=vps[:, 0:3 * CT])
             nc.gpsimd.tensor_scalar(out=keepc[:], in0=vcol[:, 2 * CT:3 * CT], scalar1=P_KEEP, scalar2=None, op0=ALU.is_lt)
+            nc.gpsimd.tensor_scalar(out=keepe[:], in0=keepc[:], scalar1=INV_EPS, scalar2=None, op0=ALU.mult)
             nc.gpsimd.tensor_tensor(out=b1k[:], in0=b1c, in1=keepc[:], op=ALU.mult)
 
         wcodes = []
@@ -256,10 +258,8 @@ def tile_splitnn_pa_kernel(tc, x1, x2_bytes, x2_scale, W1, b1, W2, b2, noise_std
             ext = keep.tile([P, 2], F32, name="ext")
             nc.vector.tensor_reduce(out=ext[:, 0:1], in_=spread[:, 0, :], axis=AX.X, op=ALU.max)
             nc.vector.tensor_reduce(out=ext[:, 1:2], in_=spread[:, 1, :], axis=AX.X, op=ALU.min)
-            mul = keep.tile([P, 1], F32, name="mul")
-            nc.vector.tensor_scalar(out=mul[:], in0=ext[:, 0:1], scalar1=ext[:, 1:2], scalar2=INV_EPS,
-                                    op0=ALU.subtract, op1=ALU.mult)
-            nc.vector.tensor_scalar(out=mulk[:], in0=keepc[:], scalar1=mul[:, 0:1], scalar2=None, op0=ALU.mult)
+            nc.vector.scalar_tensor_tensor(out=mulk[:], in0=ext[:, 0:1].to_broadcast([P, CT]), scalar=ext[:, 1:2], in1=keepe[:],
+                                           op0=ALU.subtract, op1=ALU.mult)
 
         nT = {}
         cT = {}
@@ -282,9 +282,21 @@ def tile_splitnn_pa_kernel(tc, x1, x2_bytes, x2_scale, W1, b1, W2, b2, noise_std
             nT[(h, c0 + 1)] = t[:, 1, :]
 
         def c_make(h, c):
-            t = rot.tile([P, HALF], F32, name="cT", tag="cT", bufs=8)
+            t = rot.tile([P, HALF], F32, name="cT", tag="cT", bufs=CT)
             nc.vector.scalar_tensor_tensor(out=t[:], in0=nT[(h, c)], scalar=mulk[:, c:c + 1], in1=akT[(h, c)][:],
                                            op0=ALU.mult, op1=ALU.add)
+            cT[(h, c)] = t
+
+        nm = {}
+
+        def n_mul(h, c):
+            t = keep.tile([P, HALF], F32, name="nm%d%d" % (h, c))
+            nc.scalar.activation(out=t[:], in_=nT[(h, c)], func=ACT.Copy, scale=mulk[:, c:c + 1])
+            nm[(h, c)] = t
+
+        def c_add(h, c):
+            t = keep.tile([P, HALF], F32, name="cg%d%d" % (h, c))
+            nc.gpsimd.tensor_tensor(out=t[:], in0=nm[(h, c)][:], in1=akT[(h, c)][:], op=ALU.add)
             cT[(h, c)] = t
 
         def o_make(h, c, q=0, n=HALF):
@@ -384,19 +396,25 @@ def tile_splitnn_pa_kernel(tc, x1, x2_bytes, x2_scale, W1, b1, W2, b2, noise_std
         c_make(0, 1)
         c_make(0, 2)
         c_make(0, 3)
-        for c in range(CT):
-            mx(1, 0, c)
         c1_keep(1, 2)
         c1_keep(1, 3)
         noise_turn(1, 0)
         noise_turn(1, 2)
+        n_mul(1, 0)
+        c_add(1, 0)
+        n_mul(1, 1)
+        c_add(1, 1)
+        n_mul(1, 2)
+        c_add(1, 2)
+        n_mul(1, 3)
+        c_add(1, 3)
+        for c in range(CT):
+            mx(1, 0, c)
         x_quant(1, 1)
         for c in range(CT):
             o_make(0, c)
         mx(1, 1, 0)
         mx(1, 1, 1)
-        for c in range(CT):
-            c_make(1, c)
         for i in range(RT):
             o_turn(0, i, range(CT))
             o_out(0, i, "S")

@@ -46,8 +46,6 @@ def tile_splitnn_pa_kernel(tc, x1, x2_bytes, x2_scale, W1, b1, W2, b2, noise_std
         nz_v = noise_std.rearrange("(p a) c -> p a c", a=NT)
         out_v = out.rearrange("(p a) c -> p a c", a=NT)
 
-        srow = keep.tile([P, P], F32, name="srow")
-        nc.gpsimd.memset(srow[:], 0.0)
         vrow = keep.tile([P, P], BF16, name="vrow")
         nc.gpsimd.memset(vrow[:], 0.0)
         warm = keep.tile([P, 2], F32, name="warm")
@@ -59,6 +57,7 @@ def tile_splitnn_pa_kernel(tc, x1, x2_bytes, x2_scale, W1, b1, W2, b2, noise_std
         make_identity(nc, ident_b[:])
 
         weights = (W1, W2)
+        scl = keep.tile([P, PASSES, PACK], F32, name="scl")
         wraw = {}
         x1sb = keep.tile([P, NT, K], BF16, name="x1sb")
         xbytes = keep.tile([P, NT, K], U8, name="x2bytes")
@@ -79,7 +78,6 @@ def tile_splitnn_pa_kernel(tc, x1, x2_bytes, x2_scale, W1, b1, W2, b2, noise_std
             nc.sync.dma_start(out=noise[:, a:a + n, :], in_=nz_v[:, a:a + n, :])
 
         def load_small():
-            nc.sync.dma_start(out=srow[0:K // P, :], in_=x2_scale.rearrange("o (j n) -> (o j) n", n=P))
             for j, vec in enumerate((b1, b2, rr_uniform)):
                 nc.sync.dma_start(out=vrow[CT * j:CT * (j + 1), :], in_=vec.rearrange("(c p) -> c p", p=P))
 
@@ -89,6 +87,7 @@ def tile_splitnn_pa_kernel(tc, x1, x2_bytes, x2_scale, W1, b1, W2, b2, noise_std
         load_x1(0, 2)
         load_x1(2, 2)
         load_w(0, 1)
+        nc.sync.dma_start(out=scl[:], in_=x2_scale.rearrange("o (g p t) -> p (o g) t", p=P, t=PACK))
         load_x1(4, 2)
         load_x1(6, 1)
         load_x1(7, 1)
@@ -97,20 +96,6 @@ def tile_splitnn_pa_kernel(tc, x1, x2_bytes, x2_scale, W1, b1, W2, b2, noise_std
         load_w(1, 1)
         load_noise(0, 4)
         load_noise(4, 4)
-
-        scale_bc = keep.tile([P, K], F32, name="scale_bc")
-        scol = keep.tile([P, K // P], F32, name="scol")
-
-        def scale_cols():
-            t = bank([P, P], F32)
-            nc.tensor.transpose(t[:], srow[:], ident_f[:])
-            nc.scalar.copy(out=scol[:], in_=t[:, 0:K // P])
-
-        def scale_spread(s):
-            t = bank([P, RT, P], F32)
-            for j in range(RT):
-                nc.tensor.transpose(t[:, j, :], scol[:, s * RT + j:s * RT + j + 1].to_broadcast([P, P]), ident_f[:])
-            nc.scalar.copy(out=scale_bc[:, s * HALF:(s + 1) * HALF], in_=t[:].rearrange("p j n -> p (j n)"))
 
         vcol = keep.tile([P, 3 * CT], F32, name="vcol")
         b1c = vcol[:, 0:CT]
@@ -165,13 +150,23 @@ def tile_splitnn_pa_kernel(tc, x1, x2_bytes, x2_scale, W1, b1, W2, b2, noise_std
         xt = {}
         x2bf = keep.tile([P, NT, K], BF16, name="x2bf")
 
-        def widen(a):
-            nc.vector.tensor_tensor(out=x2bf[:, a, :], in0=xbytes[:, a, :].bitcast(FP8), in1=scale_bc[:], op=ALU.mult)
+        def cast(a, eng):
+            if eng == "S":
+                nc.scalar.copy(out=x2bf[:, a, :], in_=xbytes[:, a, :].bitcast(FP8))
+            elif eng == "V":
+                nc.vector.tensor_copy(out=x2bf[:, a, :], in_=xbytes[:, a, :].bitcast(FP8))
+            else:
+                nc.gpsimd.tensor_copy(out=x2bf[:, a, :], in_=xbytes[:, a, :].bitcast(FP8))
 
-        def x_turn(w, a):
+        def kick(t, n):
+            for j in range(n):
+                nc.tensor.matmul(out=t, lhsT=ident_f[:], rhs=ident_f[:])
+
+        def x_turn(w, a, n=0):
             src = x1sb if w == 0 else x2bf
             words = src[:, a, :].bitcast(F32)
             t = bank([P, PASSES, 2, P], F32)
+            kick(t[:, 1, 1, :], n)
             for g in range(PASSES):
                 for u in range(2):
                     nc.tensor.transpose(t[:, g, u, :], words[:, 256 * g + u:256 * (g + 1):2], ident_f[:])
@@ -185,6 +180,14 @@ def tile_splitnn_pa_kernel(tc, x1, x2_bytes, x2_scale, W1, b1, W2, b2, noise_std
                 nc.vector.tensor_copy(out=dst, in_=src)
             else:
                 nc.scalar.copy(out=dst, in_=src)
+
+        def x_scale(a):
+            h, i = divmod(a, RT)
+            for g in range(PASSES):
+                nc.vector.tensor_tensor(out=xgrp[(1, h)][:, g, i * P:(i + 1) * P, :].rearrange("p r (u e) -> p r u e", e=2),
+                                        in0=xt[(1, a)][:, g, :, :].bitcast(BF16).rearrange("p u (r e) -> p r u e", e=2),
+                                        in1=scl[:, g, :].rearrange("p (u e) -> p u e", e=2).unsqueeze(1).to_broadcast([P, P, 2, 2]),
+                                        op=ALU.mult)
 
         def x_quant(w, h):
             nc.vector.quantize_mx(out=xcodes[(w, h)][:].rearrange("p g r -> p (g r)").bitcast(FP8X4),
@@ -282,7 +285,7 @@ def tile_splitnn_pa_kernel(tc, x1, x2_bytes, x2_scale, W1, b1, W2, b2, noise_std
             nT[(h, c0 + 1)] = t[:, 1, :]
 
         def c_make(h, c):
-            t = rot.tile([P, HALF], F32, name="cT", tag="cT", bufs=CT)
+            t = rot.tile([P, HALF], F32, name="cT", tag="cT", bufs=8)
             nc.vector.scalar_tensor_tensor(out=t[:], in0=nT[(h, c)], scalar=mulk[:, c:c + 1], in1=akT[(h, c)][:],
                                            op0=ALU.mult, op1=ALU.add)
             cT[(h, c)] = t
@@ -290,12 +293,12 @@ def tile_splitnn_pa_kernel(tc, x1, x2_bytes, x2_scale, W1, b1, W2, b2, noise_std
         nm = {}
 
         def n_mul(h, c):
-            t = keep.tile([P, HALF], F32, name="nm%d%d" % (h, c))
+            t = rot.tile([P, HALF], F32, name="nm", tag="nm", bufs=CT)
             nc.scalar.activation(out=t[:], in_=nT[(h, c)], func=ACT.Copy, scale=mulk[:, c:c + 1])
             nm[(h, c)] = t
 
         def c_add(h, c):
-            t = keep.tile([P, HALF], F32, name="cg%d%d" % (h, c))
+            t = rot.tile([P, HALF], F32, name="cT", tag="cT", bufs=8)
             nc.gpsimd.tensor_tensor(out=t[:], in0=nm[(h, c)][:], in1=akT[(h, c)][:], op=ALU.add)
             cT[(h, c)] = t
 
@@ -328,80 +331,67 @@ def tile_splitnn_pa_kernel(tc, x1, x2_bytes, x2_scale, W1, b1, W2, b2, noise_std
             nc.sync.dma_start(out=out_v[:, a:a + n, :], in_=osb[a // 2][:, a % 2:a % 2 + n, :])
 
         w_lace(0, 0, "V")
-        scale_cols()
-        scale_spread(0)
-        scale_spread(1)
         w_quant(0, 0)
-        widen(0)
-        widen(1)
-        widen(2)
-        for a in range(NT):
-            x_turn(0, a)
         for a in range(RT):
-            x_copy(0, a)
-        w_lace(0, 1, "V")
-        x_quant(0, 0)
-        w_quant(0, 1)
-        for a in range(RT, NT):
-            x_copy(0, a)
+            cast(a, "S" if a < 2 else "G")
+        for a in range(NT):
+            x_turn(0, a, 6 if a == 0 else 0)
+        for a in range(NT):
+            x_copy(0, a, "V" if a < 2 else "S")
         vec_prep()
-        widen(3)
+        for a in range(RT, NT):
+            cast(a, "G")
+        w_lace(0, 1, "V")
+        w_quant(0, 1)
+        x_quant(0, 0)
         x_quant_rows(0, 1, 0, 2 * P)
         x_quant_rows(0, 1, 2 * P, 2 * P)
         for c in range(CT):
             mx(0, 0, c)
-        c1_abs(0, 0)
-        c1_keep(0, 0)
-        c1_abs(0, 1)
-        w_lace(1, 0, "S", 0, P)
-        c1_keep(0, 1)
-        c1_abs(0, 2)
-        c1_abs(0, 3)
-        w_lace(1, 0, "S", P, P)
-        widen(4)
-        w_lace(1, 1, "V")
-        c1_keep(0, 2, "V")
+        for c in range(CT):
+            c1_abs(0, c)
+            c1_keep(0, c)
+        x_turn(1, 0)
+        x_turn(1, 1)
         for c in range(CT):
             mx(0, 1, c)
+        w_lace(1, 0, "V")
+        x_scale(0)
+        x_scale(1)
+        x_turn(1, 2)
+        x_turn(1, 3)
         norm_turn(0)
+        x_scale(2)
+        x_scale(3)
         for c in range(CT):
             c1_abs(1, c)
-            if c % 2 == 1:
-                w_lace(1, 0, "S", (c + 3) // 2 * P, P)
-        widen(5)
-        widen(6)
         norm_sum(0)
         norm_turn(1)
-        widen(7)
-        c1_keep(0, 3)
-        c1_keep(1, 0)
-        c1_keep(1, 1)
-        for a in range(RT):
-            x_turn(1, a)
+        for c in range(CT):
+            c1_keep(1, c)
+        x_quant(1, 0)
         norm_sum(1)
         barrier_a()
         w_quant(1, 0)
-        w_quant(1, 1)
-        for a in range(RT):
-            x_copy(1, a)
+        x_turn(1, 4)
+        x_turn(1, 5)
         noise_turn(0, 0)
         noise_turn(0, 2)
+        x_turn(1, 6)
+        x_turn(1, 7)
         barrier_b()
-        c_make(0, 0)
-        x_quant(1, 0)
-        for a in range(RT, NT):
-            x_turn(1, a)
-        for a in range(RT, NT):
-            x_copy(1, a)
-        c_make(0, 1)
-        c_make(0, 2)
-        c_make(0, 3)
-        c1_keep(1, 2)
-        c1_keep(1, 3)
+        w_lace(1, 1, "S")
+        x_scale(4)
+        n_mul(0, 2)
+        c_add(0, 2)
+        n_mul(0, 3)
+        c_add(0, 3)
+        x_scale(5)
+        w_quant(1, 1)
+        x_scale(6)
+        x_scale(7)
         noise_turn(1, 0)
         noise_turn(1, 2)
-        n_mul(1, 0)
-        c_add(1, 0)
         n_mul(1, 1)
         c_add(1, 1)
         n_mul(1, 2)
@@ -411,23 +401,22 @@ def tile_splitnn_pa_kernel(tc, x1, x2_bytes, x2_scale, W1, b1, W2, b2, noise_std
         for c in range(CT):
             mx(1, 0, c)
         x_quant(1, 1)
+        c_make(0, 0)
+        c_make(0, 1)
         for c in range(CT):
             o_make(0, c)
-        mx(1, 1, 0)
-        mx(1, 1, 1)
+        c_make(1, 0)
+        for c in range(CT):
+            mx(1, 1, c)
         for i in range(RT):
             o_turn(0, i, range(CT))
             o_out(0, i, "S")
-            if i % 2 == 1:
-                o_store(i - 1, 2)
-        mx(1, 1, 2)
-        mx(1, 1, 3)
+            o_store(i, 1)
         for q in range(2):
             for c in range(CT):
                 o_make(1, c, q, 256)
                 o_turn(1, 2 * q, [c])
                 o_turn(1, 2 * q + 1, [c])
-            o_out(1, 2 * q, "S")
-            o_store(RT + 2 * q, 1)
-            o_out(1, 2 * q + 1, "S" if q == 0 else "V")
-            o_store(RT + 2 * q + 1, 1)
+        for i in range(RT):
+            o_out(1, i, "V" if i in (3,) else "S")
+            o_store(RT + i, 1)

@@ -140,6 +140,8 @@ def tile_splitnn_pa_kernel(tc, x1, x2_bytes, x2_scale, W1, b1, W2, b2, noise_std
             dst = wgrp[(w, g)][:, c0:c0 + n, :].rearrange("p (c i) j -> p c j i", i=4)
             if eng == "V":
                 nc.vector.tensor_copy(out=dst, in_=src)
+            elif eng == "G":
+                nc.gpsimd.tensor_copy(out=dst, in_=src)
             else:
                 nc.scalar.copy(out=dst, in_=src)
 
@@ -188,6 +190,19 @@ def tile_splitnn_pa_kernel(tc, x1, x2_bytes, x2_scale, W1, b1, W2, b2, noise_std
                                         in0=xt[(1, a)][:, g, :, :].bitcast(BF16).rearrange("p u (r e) -> p r u e", e=2),
                                         in1=scl[:, g, :].rearrange("p (u e) -> p u e", e=2).unsqueeze(1).to_broadcast([P, P, 2, 2]),
                                         op=ALU.mult)
+
+        xraw = {}
+
+        def x_raw(a):
+            t = rot.tile([P, PASSES, P, PACK], BF16, name="xraw", tag="xraw", bufs=2, align_bytes=64)
+            nc.scalar.copy(out=t[:].bitcast(F32), in_=xt[(1, a)][:].rearrange("p g u r -> p g r u"))
+            xraw[a] = t
+
+        def g_scale(a):
+            h, i = divmod(a, RT)
+            for g in range(PASSES):
+                nc.gpsimd.tensor_tensor(out=xgrp[(1, h)][:, g, i * P:(i + 1) * P, :], in0=xraw[a][:, g, :, :],
+                                        in1=scl[:, g, :].unsqueeze(1).to_broadcast([P, P, PACK]), op=ALU.mult)
 
         def x_quant(w, h):
             nc.vector.quantize_mx(out=xcodes[(w, h)][:].rearrange("p g r -> p (g r)").bitcast(FP8X4),
@@ -335,7 +350,7 @@ def tile_splitnn_pa_kernel(tc, x1, x2_bytes, x2_scale, W1, b1, W2, b2, noise_std
         for a in range(RT):
             cast(a, "S" if a < 2 else "G")
         for a in range(NT):
-            x_turn(0, a, 6 if a == 0 else 0)
+            x_turn(0, a, 13 if a == 0 else 0)
         for a in range(NT):
             x_copy(0, a, "V" if a < 2 else "S")
         vec_prep()
@@ -363,8 +378,14 @@ def tile_splitnn_pa_kernel(tc, x1, x2_bytes, x2_scale, W1, b1, W2, b2, noise_std
         norm_turn(0)
         x_scale(2)
         x_scale(3)
+        x_turn(1, 4)
+        x_turn(1, 5)
         for c in range(CT):
             c1_abs(1, c)
+        x_raw(4)
+        g_scale(4)
+        x_raw(5)
+        g_scale(5)
         norm_sum(0)
         norm_turn(1)
         for c in range(CT):
@@ -373,23 +394,19 @@ def tile_splitnn_pa_kernel(tc, x1, x2_bytes, x2_scale, W1, b1, W2, b2, noise_std
         norm_sum(1)
         barrier_a()
         w_quant(1, 0)
-        x_turn(1, 4)
-        x_turn(1, 5)
-        noise_turn(0, 0)
-        noise_turn(0, 2)
         x_turn(1, 6)
         x_turn(1, 7)
+        noise_turn(0, 0)
+        noise_turn(0, 2)
         barrier_b()
         w_lace(1, 1, "S")
-        x_scale(4)
+        x_scale(6)
         n_mul(0, 2)
         c_add(0, 2)
         n_mul(0, 3)
         c_add(0, 3)
-        x_scale(5)
-        w_quant(1, 1)
-        x_scale(6)
         x_scale(7)
+        w_quant(1, 1)
         noise_turn(1, 0)
         noise_turn(1, 2)
         n_mul(1, 1)
@@ -403,15 +420,17 @@ def tile_splitnn_pa_kernel(tc, x1, x2_bytes, x2_scale, W1, b1, W2, b2, noise_std
         x_quant(1, 1)
         c_make(0, 0)
         c_make(0, 1)
-        for c in range(CT):
-            o_make(0, c)
+        for q in range(2):
+            for c in range(CT):
+                o_make(0, c, q, 256)
         c_make(1, 0)
-        for c in range(CT):
-            mx(1, 1, c)
-        for i in range(RT):
-            o_turn(0, i, range(CT))
-            o_out(0, i, "S")
-            o_store(i, 1)
+        for q in range(2):
+            mx(1, 1, 2 * q)
+            mx(1, 1, 2 * q + 1)
+            for i in (2 * q, 2 * q + 1):
+                o_turn(0, i, range(CT))
+                o_out(0, i, "S")
+                o_store(i, 1)
         for q in range(2):
             for c in range(CT):
                 o_make(1, c, q, 256)

@@ -83,14 +83,15 @@ def tile_splitnn_pa_kernel(tc, x1, x2_bytes, x2_scale, W1, b1, W2, b2, noise_std
 
         load_small()
         load_w(0, 0)
-        load_bytes(0, 4)
+        load_w(0, 1)
+        load_bytes(0, 2)
         load_x1(0, 2)
         load_x1(2, 2)
-        load_w(0, 1)
         nc.sync.dma_start(out=scl[:], in_=x2_scale.rearrange("o (g p t) -> p (o g) t", p=P, t=PACK))
         load_x1(4, 2)
         load_x1(6, 1)
         load_x1(7, 1)
+        load_bytes(2, 2)
         load_bytes(4, 4)
         load_w(1, 0)
         load_w(1, 1)
@@ -347,17 +348,18 @@ def tile_splitnn_pa_kernel(tc, x1, x2_bytes, x2_scale, W1, b1, W2, b2, noise_std
 
         w_lace(0, 0, "V")
         w_quant(0, 0)
-        for a in range(RT):
-            cast(a, "S" if a < 2 else "G")
+        w_lace(0, 1, "V")
+        w_quant(0, 1)
+        cast(0, "S")
+        cast(1, "S")
+        cast(2, "G")
         for a in range(NT):
             x_turn(0, a, 13 if a == 0 else 0)
         for a in range(NT):
             x_copy(0, a, "V" if a < 2 else "S")
         vec_prep()
-        for a in range(RT, NT):
+        for a in range(3, NT):
             cast(a, "G")
-        w_lace(0, 1, "V")
-        w_quant(0, 1)
         x_quant(0, 0)
         x_quant_rows(0, 1, 0, 2 * P)
         x_quant_rows(0, 1, 2 * P, 2 * P)
@@ -373,6 +375,7 @@ def tile_splitnn_pa_kernel(tc, x1, x2_bytes, x2_scale, W1, b1, W2, b2, noise_std
         w_lace(1, 0, "V")
         x_scale(0)
         x_scale(1)
+        w_quant(1, 0)
         x_turn(1, 2)
         x_turn(1, 3)
         norm_turn(0)
@@ -388,19 +391,20 @@ def tile_splitnn_pa_kernel(tc, x1, x2_bytes, x2_scale, W1, b1, W2, b2, noise_std
         g_scale(5)
         norm_sum(0)
         norm_turn(1)
-        for c in range(CT):
-            c1_keep(1, c)
+        c1_keep(1, 0)
+        c1_keep(1, 1)
+        w_lace(1, 1, "S")
+        c1_keep(1, 2)
+        c1_keep(1, 3)
         x_quant(1, 0)
         norm_sum(1)
-        barrier_a()
-        w_quant(1, 0)
         x_turn(1, 6)
+        barrier_a()
+        x_scale(6)
         x_turn(1, 7)
         noise_turn(0, 0)
         noise_turn(0, 2)
         barrier_b()
-        w_lace(1, 1, "S")
-        x_scale(6)
         n_mul(0, 2)
         c_add(0, 2)
         n_mul(0, 3)
@@ -417,9 +421,9 @@ def tile_splitnn_pa_kernel(tc, x1, x2_bytes, x2_scale, W1, b1, W2, b2, noise_std
         c_add(1, 3)
         for c in range(CT):
             mx(1, 0, c)
-        x_quant(1, 1)
         c_make(0, 0)
         c_make(0, 1)
+        x_quant(1, 1)
         for q in range(2):
             for c in range(CT):
                 o_make(0, c, q, 256)

@@ -79,19 +79,19 @@ def tile_splitnn_pa_kernel(tc, x1, x2_bytes, x2_scale, W1, b1, W2, b2, noise_std
 
         def load_small():
             for j, vec in enumerate((b1, b2, rr_uniform)):
-                nc.sync.dma_start(out=vrow[CT * j:CT * (j + 1), :], in_=vec.rearrange("(c p) -> c p", p=P))
+                nc.scalar.dma_start(out=vrow[CT * j:CT * (j + 1), :], in_=vec.rearrange("(c p) -> c p", p=P))
+            nc.scalar.dma_start(out=scl[:], in_=x2_scale.rearrange("o (g p t) -> p (o g) t", p=P, t=PACK))
 
         load_small()
         load_w(0, 0)
         load_w(0, 1)
-        load_bytes(0, 2)
+        load_bytes(0, 1)
         load_x1(0, 2)
         load_x1(2, 2)
-        nc.sync.dma_start(out=scl[:], in_=x2_scale.rearrange("o (g p t) -> p (o g) t", p=P, t=PACK))
         load_x1(4, 2)
         load_x1(6, 1)
         load_x1(7, 1)
-        load_bytes(2, 2)
+        load_bytes(1, 3)
         load_bytes(4, 4)
         load_w(1, 0)
         load_w(1, 1)
@@ -351,14 +351,13 @@ def tile_splitnn_pa_kernel(tc, x1, x2_bytes, x2_scale, W1, b1, W2, b2, noise_std
         w_lace(0, 1, "V")
         w_quant(0, 1)
         cast(0, "S")
-        cast(1, "S")
-        cast(2, "G")
+        cast(1, "G")
         for a in range(NT):
             x_turn(0, a, 13 if a == 0 else 0)
         for a in range(NT):
-            x_copy(0, a, "V" if a < 2 else "S")
+            x_copy(0, a)
         vec_prep()
-        for a in range(3, NT):
+        for a in range(2, NT):
             cast(a, "G")
         x_quant(0, 0)
         x_quant_rows(0, 1, 0, 2 * P)
@@ -435,11 +434,11 @@ def tile_splitnn_pa_kernel(tc, x1, x2_bytes, x2_scale, W1, b1, W2, b2, noise_std
                 o_turn(0, i, range(CT))
                 o_out(0, i, "S")
                 o_store(i, 1)
-        for q in range(2):
+        for q, n, tiles in ((0, 256, (0, 1)), (2, 128, (2,)), (3, 128, (3,))):
             for c in range(CT):
-                o_make(1, c, q, 256)
-                o_turn(1, 2 * q, [c])
-                o_turn(1, 2 * q + 1, [c])
+                o_make(1, c, q, n)
+                for i in tiles:
+                    o_turn(1, i, [c])
         for i in range(RT):
             o_out(1, i, "V" if i in (3,) else "S")
             o_store(RT + i, 1)

from contextlib import ExitStack

import concourse.mybir as mybir
from concourse.masks import make_identity

ROWS, K, CH = 1024, 1024, 512
FLOPS = 2 * 2 * ROWS * K * CH

F32 = mybir.dt.float32
BF16 = mybir.dt.bfloat16
U32 = mybir.dt.uint32
U8 = mybir.dt.uint8
FP8 = mybir.dt.float8_e4m3fn
FP8X4 = mybir.dt.float8_e4m3fn_x4
ALU = mybir.AluOpType
ACT = mybir.ActivationFunctionType
AX = mybir.AxisListType

P = 128
PACK = 4
K_PASS = P * PACK
PASSES = K // K_PASS
HALF = 512
HALVES = ROWS // HALF
RT = HALF // P
CT = CH // P
NT = ROWS // P
INV_EPS = 30.0 / 4.0
P_KEEP = 0.95


def tile_splitnn_pa_kernel(tc, x1, x2_bytes, x2_scale, W1, b1, W2, b2, noise_std, rr_uniform, out):
    nc = tc.nc
    with ExitStack() as ctx:
        keep = ctx.enter_context(tc.tile_pool(name="keep", bufs=1))
        rot = ctx.enter_context(tc.tile_pool(name="rot", bufs=2))
        psum = ctx.enter_context(tc.psum_pool(name="psum", bufs=8))
        ctx.enter_context(tc.manual_schedule())

        def bank(shape, dtype):
            t = psum.tile(shape, dtype, name="bank", tag="bank", bufs=8)
            return t

        x1_v = x1.rearrange("(p a) k -> p a k", a=NT)
        xb_v = x2_bytes.rearrange("(p a) k -> p a k", a=NT)
        nz_v = noise_std.rearrange("(p a) c -> p a c", a=NT)
        out_v = out.rearrange("(p a) c -> p a c", a=NT)

        vrow = keep.tile([P, P], BF16, name="vrow")
        nc.gpsimd.memset(vrow[:], 0.0)
        warm = keep.tile([P, 2], F32, name="warm")
        nc.vector.memset(warm[:], 0.0)
        nc.scalar.activation(out=warm[:, 1:2], in_=warm[:, 0:1], func=ACT.Abs)
        ident_f = keep.tile([P, P], F32, name="ident_f")
        make_identity(nc, ident_f[:])
        ident_b = keep.tile([P, P], BF16, name="ident_b")
        make_identity(nc, ident_b[:])

        weights = (W1, W2)
        scl = keep.tile([P, PASSES, PACK], F32, name="scl")
        wraw = {}
        x1sb = keep.tile([P, NT, K], BF16, name="x1sb")
        xbytes = keep.tile([P, NT, K], U8, name="x2bytes")
        noise = keep.tile([P, NT, CH], BF16, name="noise")

        def load_w(w, g):
            t = keep.tile([P, PACK, CH], BF16, name="wraw%d%d" % (w, g))
            wraw[(w, g)] = t
            nc.sync.dma_start(out=t[:], in_=weights[w][g * K_PASS:(g + 1) * K_PASS, :].rearrange("(p j) c -> p j c", j=PACK))

        def load_x1(a, n):
            nc.sync.dma_start(out=x1sb[:, a:a + n, :], in_=x1_v[:, a:a + n, :])

        def load_bytes(a, n):
            nc.sync.dma_start(out=xbytes[:, a:a + n, :], in_=xb_v[:, a:a + n, :])

        def load_noise(a, n):
            nc.sync.dma_start(out=noise[:, a:a + n, :], in_=nz_v[:, a:a + n, :])

        def load_small():
            for j, vec in enumerate((b1, b2, rr_uniform)):
                nc.scalar.dma_start(out=vrow[CT * j:CT * (j + 1), :], in_=vec.rearrange("(c p) -> c p", p=P))
            nc.scalar.dma_start(out=scl[:], in_=x2_scale.rearrange("o (g p t) -> p (o g) t", p=P, t=PACK))

        load_small()
        load_w(0, 0)
        load_w(0, 1)
        load_bytes(0, 1)
        load_x1(0, 2)
        load_x1(2, 2)
        load_x1(4, 2)
        load_x1(6, 1)
        load_x1(7, 1)
        load_bytes(1, 3)
        load_bytes(4, 4)
        load_w(1, 0)
        load_w(1, 1)
        load_noise(0, 4)
        load_noise(4, 4)

        vcol = keep.tile([P, 3 * CT], F32, name="vcol")
        b1c = vcol[:, 0:CT]
        b2c = vcol[:, CT:2 * CT]
        keepc = keep.tile([P, CT], F32, name="keepc")
        b1k = keep.tile([P, CT], F32, name="b1k")
        keepe = keep.tile([P, CT], F32, name="keepe")

        def vec_prep():
            vps = bank([P, P], BF16)
            nc.tensor.transpose(vps[:], vrow[:], ident_b[:])
            nc.scalar.copy(out=vcol[:], in_=vps[:, 0:3 * CT])
            nc.gpsimd.tensor_scalar(out=keepc[:], in0=vcol[:, 2 * CT:3 * CT], scalar1=P_KEEP, scalar2=None, op0=ALU.is_lt)
            nc.gpsimd.tensor_scalar(out=keepe[:], in0=keepc[:], scalar1=INV_EPS, scalar2=None, op0=ALU.mult)
            nc.gpsimd.tensor_tensor(out=b1k[:], in0=b1c, in1=keepc[:], op=ALU.mult)

        wcodes = []
        wscl = []
        wgrp = {}
        for w in range(2):
            wc = keep.tile([P, PASSES, CH], U32, name="wcodes%d" % w, align_bytes=64)
            ws = keep.tile([P, PASSES, CH], U8, name="wscl%d" % w, align_bytes=64)
            wcodes.append(wc)
            wscl.append(ws)
            for g in range(PASSES):
                wg = keep.tile([P, CH, PACK], BF16, name="wgrp%d%d" % (w, g), align_bytes=64)
                wgrp[(w, g)] = wg
        xgrp = {}
        xcodes = {}
        xscl = {}
        for w in range(2):
            for h in range(HALVES):
                xg = keep.tile([P, PASSES, HALF, PACK], BF16, name="xgrp%d%d" % (w, h), align_bytes=64)
                xc = keep.tile([P, PASSES, HALF], U32, name="xcodes%d%d" % (w, h), align_bytes=64)
                xs = keep.tile([P, PASSES, HALF], U8, name="xscl%d%d" % (w, h), align_bytes=64)
                xgrp[(w, h)] = xg
                xcodes[(w, h)] = xc
                xscl[(w, h)] = xs

        def w_lace(w, g, eng, c0=0, n=CH):
            src = wraw[(w, g)][:, :, c0:c0 + n].rearrange("p j (c i) -> p c j i", i=4)
            dst = wgrp[(w, g)][:, c0:c0 + n, :].rearrange("p (c i) j -> p c j i", i=4)
            if eng == "V":
                nc.vector.tensor_copy(out=dst, in_=src)
            elif eng == "G":
                nc.gpsimd.tensor_copy(out=dst, in_=src)
            else:
                nc.scalar.copy(out=dst, in_=src)

        def w_quant(w, g):
            nc.vector.quantize_mx(out=wcodes[w][:, g, :].bitcast(FP8X4), scales=wscl[w][:, g, :],
                                  in_=wgrp[(w, g)][:].rearrange("p c j -> p (c j)"))

        xt = {}
        x2bf = keep.tile([P, NT, K], BF16, name="x2bf")

        def cast(a, eng):
            if eng == "S":
                nc.scalar.copy(out=x2bf[:, a, :], in_=xbytes[:, a, :].bitcast(FP8))
            elif eng == "V":
                nc.vector.tensor_copy(out=x2bf[:, a, :], in_=xbytes[:, a, :].bitcast(FP8))
            else:
                nc.gpsimd.tensor_copy(out=x2bf[:, a, :], in_=xbytes[:, a, :].bitcast(FP8))

        def kick(t, n):
            for j in range(n):
                nc.tensor.matmul(out=t, lhsT=ident_f[:], rhs=ident_f[:])

        def x_turn(w, a, n=0):
            src = x1sb if w == 0 else x2bf
            words = src[:, a, :].bitcast(F32)
            t = bank([P, PASSES, 2, P], F32)
            kick(t[:, 1, 1, :], n)
            for g in range(PASSES):
                for u in range(2):
                    nc.tensor.transpose(t[:, g, u, :], words[:, 256 * g + u:256 * (g + 1):2], ident_f[:])
            xt[(w, a)] = t

        def x_copy(w, a, eng="S"):
            h, i = divmod(a, RT)
            dst = xgrp[(w, h)][:].bitcast(F32)[:, :, i * P:(i + 1) * P, :]
            src = xt[(w, a)][:].rearrange("p g u r -> p g r u")
            if eng == "V":
                nc.vector.tensor_copy(out=dst, in_=src)
            else:
                nc.scalar.copy(out=dst, in_=src)

        def x_scale(a):
            h, i = divmod(a, RT)
            for g in range(PASSES):
                nc.vector.tensor_tensor(out=xgrp[(1, h)][:, g, i * P:(i + 1) * P, :].rearrange("p r (u e) -> p r u e", e=2),
                                        in0=xt[(1, a)][:, g, :, :].bitcast(BF16).rearrange("p u (r e) -> p r u e", e=2),
                                        in1=scl[:, g, :].rearrange("p (u e) -> p u e", e=2).unsqueeze(1).to_broadcast([P, P, 2, 2]),
                                        op=ALU.mult)

        xraw = {}

        def x_raw(a):
            t = rot.tile([P, PASSES, P, PACK], BF16, name="xraw", tag="xraw", bufs=2, align_bytes=64)
            nc.scalar.copy(out=t[:].bitcast(F32), in_=xt[(1, a)][:].rearrange("p g u r -> p g r u"))
            xraw[a] = t

        def g_scale(a):
            h, i = divmod(a, RT)
            for g in range(PASSES):
                nc.gpsimd.tensor_tensor(out=xgrp[(1, h)][:, g, i * P:(i + 1) * P, :], in0=xraw[a][:, g, :, :],
                                        in1=scl[:, g, :].unsqueeze(1).to_broadcast([P, P, PACK]), op=ALU.mult)

        def x_quant(w, h):
            nc.vector.quantize_mx(out=xcodes[(w, h)][:].rearrange("p g r -> p (g r)").bitcast(FP8X4),
                                  scales=xscl[(w, h)][:].rearrange("p g r -> p (g r)"),
                                  in_=xgrp[(w, h)][:].rearrange("p g r t -> p (g r t)"))

        def x_quant_rows(w, h, r0, n):
            for g in range(PASSES):
                nc.vector.quantize_mx(out=xcodes[(w, h)][:, g, r0:r0 + n].bitcast(FP8X4), scales=xscl[(w, h)][:, g, r0:r0 + n],
                                      in_=xgrp[(w, h)][:, g, r0:r0 + n, :].rearrange("p r t -> p (r t)"))

        acc = {}

        def mx(w, h, c):
            t = bank([P, HALF], F32)
            for g in range(PASSES):
                nc.tensor.matmul_mx(out=t[:],
                                    lhsT=wcodes[w][:, g, c * P:(c + 1) * P].bitcast(FP8X4),
                                    lhsT_scale=wscl[w][:, g, c * P:(c + 1) * P],
                                    rhs=xcodes[(w, h)][:, g, :].bitcast(FP8X4),
                                    rhs_scale=xscl[(w, h)][:, g, :],
                                    start=(g == 0), stop=(g == PASSES - 1))
            acc[(w, h, c)] = t

        absT = {}
        akT = {}

        def c1_abs(h, c):
            ab = rot.tile([P, HALF], F32, name="absT", tag="absT", bufs=8)
            nc.scalar.activation(out=ab[:], in_=acc[(0, h, c)][:], func=ACT.Abs, bias=b1c[:, c:c + 1], scale=1.0)
            absT[(h, c)] = ab

        def c1_keep(h, c, eng="S"):
            ak = keep.tile([P, HALF], F32, name="akT%d%d" % (h, c))
            if eng == "V":
                nc.vector.tensor_scalar(out=ak[:], in0=acc[(0, h, c)][:], scalar1=keepc[:, c:c + 1], scalar2=b1k[:, c:c + 1],
                                        op0=ALU.mult, op1=ALU.add)
            else:
                nc.scalar.activation(out=ak[:], in_=acc[(0, h, c)][:], func=ACT.Identity, bias=b1k[:, c:c + 1],
                                     scale=keepc[:, c:c + 1])
            akT[(h, c)] = ak

        nsum = keep.tile([P, NT], F32, name="nsum")
        nps = {}

        def norm_turn(h):
            t = bank([P, RT, P], F32)
            for i in range(RT):
                for c in range(CT):
                    nc.tensor.matmul(out=t[:, i, :], lhsT=absT[(h, c)][:, i * P:(i + 1) * P], rhs=ident_f[:],
                                     is_transpose=True, start=(c == 0), stop=(c == CT - 1))
            nps[h] = t

        def norm_sum(h):
            nc.vector.tensor_reduce(out=nsum[:, h * RT:(h + 1) * RT], in_=nps[h][:], axis=AX.X, op=ALU.add)

        mulk = keep.tile([P, CT], F32, name="mulk")
        nmx = keep.tile([P, 2], F32, name="nmx")
        spr = {}

        def barrier_a():
            nc.vector.tensor_reduce(out=nmx[:, 0:1], in_=nsum[:], axis=AX.X, op=ALU.max)
            nc.vector.tensor_reduce(out=nmx[:, 1:2], in_=nsum[:], axis=AX.X, op=ALU.min)
            t = bank([P, 2, P], F32)
            for j in range(2):
                nc.tensor.transpose(t[:, j, :], nmx[:, j:j + 1].to_broadcast([P, P]), ident_f[:])
            spr[0] = t

        def barrier_b():
            spread = spr[0]
            ext = keep.tile([P, 2], F32, name="ext")
            nc.vector.tensor_reduce(out=ext[:, 0:1], in_=spread[:, 0, :], axis=AX.X, op=ALU.max)
            nc.vector.tensor_reduce(out=ext[:, 1:2], in_=spread[:, 1, :], axis=AX.X, op=ALU.min)
            nc.vector.scalar_tensor_tensor(out=mulk[:], in0=ext[:, 0:1].to_broadcast([P, CT]), scalar=ext[:, 1:2], in1=keepe[:],
                                           op0=ALU.subtract, op1=ALU.mult)

        nT = {}
        cT = {}
        oT = {}
        ob = {}
        osb = {}

        def noise_turn(h, c0):
            t = bank([P, 2, HALF], BF16)
            for c in (c0, c0 + 1):
                for i in range(RT):
                    nc.tensor.matmul(out=t[:, c - c0, i * P:(i + 1) * P], lhsT=noise[:, h * RT + i, c * P:(c + 1) * P], rhs=ident_b[:])
                nT[(h, c)] = t[:, c - c0, :]

        def noise_out(h, c0):
            t = keep.tile([P, 2, HALF], BF16, name="nsb%d%d" % (h, c0))
            nc.scalar.copy(out=t[:, 0, :], in_=nT[(h, c0)])
            nc.scalar.copy(out=t[:, 1, :], in_=nT[(h, c0 + 1)])
            nT[(h, c0)] = t[:, 0, :]
            nT[(h, c0 + 1)] = t[:, 1, :]

        def c_make(h, c):
            t = rot.tile([P, HALF], F32, name="cT", tag="cT", bufs=8)
            nc.vector.scalar_tensor_tensor(out=t[:], in0=nT[(h, c)], scalar=mulk[:, c:c + 1], in1=akT[(h, c)][:],
                                           op0=ALU.mult, op1=ALU.add)
            cT[(h, c)] = t

        nm = {}

        def n_mul(h, c):
            t = rot.tile([P, HALF], F32, name="nm", tag="nm", bufs=CT)
            nc.scalar.activation(out=t[:], in_=nT[(h, c)], func=ACT.Copy, scale=mulk[:, c:c + 1])
            nm[(h, c)] = t

        def c_add(h, c):
            t = rot.tile([P, HALF], F32, name="cT", tag="cT", bufs=8)
            nc.gpsimd.tensor_tensor(out=t[:], in0=nm[(h, c)][:], in1=akT[(h, c)][:], op=ALU.add)
            cT[(h, c)] = t

        def o_make(h, c, q=0, n=HALF):
            if (h, c) not in oT:
                t = rot.tile([P, HALF], F32, name="oT", tag="oT", bufs=8)
                oT[(h, c)] = t
            nc.vector.scalar_tensor_tensor(out=oT[(h, c)][:, q * n:(q + 1) * n], in0=acc[(1, h, c)][:, q * n:(q + 1) * n],
                                           scalar=b2c[:, c:c + 1], in1=cT[(h, c)][:, q * n:(q + 1) * n],
                                           op0=ALU.add, op1=ALU.min)

        def o_turn(h, i, cs):
            if (h, i) not in ob:
                t = bank([P, CH], F32)
                ob[(h, i)] = t
            for c in cs:
                nc.tensor.transpose(ob[(h, i)][:, c * P:(c + 1) * P], oT[(h, c)][:, i * P:(i + 1) * P], ident_f[:])

        def o_out(h, i, eng):
            a = h * RT + i
            if a // 2 not in osb:
                t = keep.tile([P, 2, CH], F32, name="osb%d" % (a // 2))
                osb[a // 2] = t
            if eng == "V":
                nc.vector.tensor_copy(out=osb[a // 2][:, a % 2, :], in_=ob[(h, i)][:])
            else:
                nc.scalar.copy(out=osb[a // 2][:, a % 2, :], in_=ob[(h, i)][:])

        def o_store(a, n):
            nc.sync.dma_start(out=out_v[:, a:a + n, :], in_=osb[a // 2][:, a % 2:a % 2 + n, :])

        w_lace(0, 0, "V")
        w_quant(0, 0)
        w_lace(0, 1, "V")
        w_quant(0, 1)
        cast(0, "S")
        cast(1, "G")
        for a in range(NT):
            x_turn(0, a, 13 if a == 0 else 0)
        for a in range(NT):
            x_copy(0, a)
        vec_prep()
        for a in range(2, NT):
            cast(a, "G")
        x_quant(0, 0)
        x_quant_rows(0, 1, 0, 2 * P)
        x_quant_rows(0, 1, 2 * P, 2 * P)
        for c in range(CT):
            mx(0, 0, c)
        for c in range(CT):
            c1_abs(0, c)
            c1_keep(0, c)
        x_turn(1, 0)
        x_turn(1, 1)
        for c in range(CT):
            mx(0, 1, c)
        w_lace(1, 0, "V")
        x_scale(0)
        x_scale(1)
        w_quant(1, 0)
        x_turn(1, 2)
        x_turn(1, 3)
        norm_turn(0)
        x_scale(2)
        x_scale(3)
        x_turn(1, 4)
        x_turn(1, 5)
        for c in range(CT):
            c1_abs(1, c)
        x_raw(4)
        g_scale(4)
        x_raw(5)
        g_scale(5)
        norm_sum(0)
        norm_turn(1)
        c1_keep(1, 0)
        c1_keep(1, 1)
        w_lace(1, 1, "S")
        c1_keep(1, 2)
        c1_keep(1, 3)
        x_quant(1, 0)
        norm_sum(1)
        x_turn(1, 6)
        barrier_a()
        x_scale(6)
        x_turn(1, 7)
        noise_turn(0, 0)
        noise_turn(0, 2)
        barrier_b()
        n_mul(0, 2)
        c_add(0, 2)
        n_mul(0, 3)
        c_add(0, 3)
        x_scale(7)
        w_quant(1, 1)
        noise_turn(1, 0)
        noise_turn(1, 2)
        n_mul(1, 1)
        c_add(1, 1)
        n_mul(1, 2)
        c_add(1, 2)
        n_mul(1, 3)
        c_add(1, 3)
        for c in range(CT):
            mx(1, 0, c)
        c_make(0, 0)
        c_make(0, 1)
        x_quant(1, 1)
        for q in range(2):
            for c in range(CT):
                o_make(0, c, q, 256)
        c_make(1, 0)
        for q in range(2):
            mx(1, 1, 2 * q)
            mx(1, 1, 2 * q + 1)
            for i in (2 * q, 2 * q + 1):
                o_turn(0, i, range(CT))
                o_out(0, i, "S")
                o_store(i, 1)
        for q, n, tiles in ((0, 256, (0, 1)), (2, 128, (2,)), (3, 128, (3,))):
            for c in range(CT):
                o_make(1, c, q, n)
                for i in tiles:
                    o_turn(1, i, [c])
        for i in range(RT):
            o_out(1, i, "V" if i in (3,) else "S")
            o_store(RT + i, 1)
